import numpy as np
import ml_dtypes


def mxq(x, axis, fmt="e4m3"):
    dtype, down = {"e4m3": (ml_dtypes.float8_e4m3fn, 7), "e5m2": (ml_dtypes.float8_e5m2, 14)}[fmt]
    v = np.moveaxis(np.asarray(x, np.float32).astype(ml_dtypes.bfloat16).astype(np.float64), axis, -1)
    blocks = v.reshape(v.shape[:-1] + (-1, 32))
    amax = np.abs(blocks).max(-1, keepdims=True)
    byte = np.maximum(np.where(amax > 0, np.frexp(amax)[1] - 1 + 127, 0) - down, 1)
    scale = np.exp2(byte - 127.0)
    codes = (blocks / scale).astype(np.float32).astype(dtype).astype(np.float64)
    return np.moveaxis((codes * scale).reshape(v.shape), -1, axis)


WIDE = False


def mx_kscale(k):
    if not WIDE:
        return np.ones(k)
    levels = np.array([20, -20, 10, -10, 0])
    a = np.random.permutation(np.resize(levels, k // 512 * 4)).reshape(k // 512, 4)
    idx = np.arange(k)
    return np.exp2(a[idx // 512, idx % 128 // 32])


BF16 = ml_dtypes.bfloat16


def bf(x):
    return np.asarray(x, np.float32).astype(BF16)


def f64(x):
    return np.asarray(x).astype(np.float64)


N, D, P, G = 1536, 256, 8, 16
EPS = 1e-12
EPSILON = 0.65


def unit_rows(features, weight_tensor):
    context = features[None, :, :] * weight_tensor[:, None, :]
    nrm = np.maximum(np.sqrt((context ** 2).sum(-1, keepdims=True)), EPS)
    return context / nrm, nrm


def as_matrix(c):
    return c.transpose(1, 0, 2).reshape(N, P * D)


def setup_inputs():
    s = mx_kscale(N)
    a = s.reshape(N // 512, 16, 32).transpose(1, 0, 2).reshape(N)
    centres = np.random.standard_normal((G, D))
    which = np.random.randint(0, G, N)
    f0 = bf(centres[which] + 0.4 * np.random.standard_normal((N, D)))
    limit = np.sqrt(6.0 / (P + D))
    w = bf(np.random.uniform(-limit, limit, (P, D)))
    g = np.random.standard_normal((N, N)) * np.exp2(np.random.randint(-12, 1, (N, 1))) * 64.0
    cm = as_matrix(unit_rows(f64(f0), f64(w))[0])
    similarity = cm @ cm.T / P
    return {"features": bf(f64(f0) * a[:, None]), "weight_tensor": w,
            "similarity": np.asarray(similarity, np.float32),
            "grad_out": bf(g * a[:, None] * a[None, :])}


def reference(features, weight_tensor, similarity, grad_out):
    w = f64(weight_tensor)
    c, nrm = unit_rows(f64(features), w)
    g = f64(grad_out)
    h = np.where(f64(similarity) > EPSILON, g + g.T, 0.0)
    dc = (mxq(h, 1, "e5m2") @ mxq(as_matrix(c), 0, "e4m3")) / P
    dc = dc.reshape(N, P, D).transpose(1, 0, 2)
    dctx = (dc - c * (dc * c).sum(-1, keepdims=True)) / nrm
    return (dctx * w[:, None, :]).sum(0)

@@ -1,0 +1,340 @@
+from contextlib import ExitStack
+
+import concourse.mybir as mybir
+from concourse.masks import make_identity
+
+FLOPS = 2 * 1536 * 1536 * 2048
+
+BF16 = mybir.dt.bfloat16
+F32 = mybir.dt.float32
+U32 = mybir.dt.uint32
+U8 = mybir.dt.uint8
+E4M3X4 = mybir.dt.float8_e4m3fn_x4
+E5M2X4 = mybir.dt.float8_e5m2_x4
+ALU = mybir.AluOpType
+ACT = mybir.ActivationFunctionType
+
+P = 128
+PACK = 4
+TOKENS = 1536
+TILES = TOKENS // P
+PASSES = TOKENS // (P * PACK)
+FEATURES = 256
+HALVES = FEATURES // P
+VIEWS = 8
+COLUMNS = VIEWS * FEATURES
+BANK = 512
+BANKS = COLUMNS // BANK
+VIEWS_PER_BANK = BANK // FEATURES
+THRESHOLD = 0.65
+EPS = 1e-12
+SIM_AHEAD = 3
+
+
+def tile_graphlearner_v_kernel(tc, features, weight_tensor, similarity, grad_out, out):
+    nc = tc.nc
+    with ExitStack() as stack:
+        keep = stack.enter_context(tc.tile_pool(name="keep", bufs=1))
+        c_stage = stack.enter_context(tc.tile_pool(name="c_stage", bufs=2))
+        sim_pool = stack.enter_context(tc.tile_pool(name="sim_pool", bufs=SIM_AHEAD))
+        h_stage = stack.enter_context(tc.tile_pool(name="h_stage", bufs=2))
+        e_stage = stack.enter_context(tc.tile_pool(name="e_stage", bufs=2))
+        ps_bank = stack.enter_context(tc.psum_pool(name="ps_bank", bufs=5))
+        ps_half = stack.enter_context(tc.psum_pool(name="ps_half", bufs=2))
+        ps_small = stack.enter_context(tc.psum_pool(name="ps_small", bufs=1))
+
+        warm = keep.tile([P, 1], F32)
+        nc.vector.memset(warm[:], 1.0)
+        nc.scalar.activation(out=warm[:], in_=warm[:], func=ACT.Sqrt)
+
+        f_bf = keep.tile([P, TILES, FEATURES], BF16)
+        nc.sync.dma_start(out=f_bf[:], in_=features.rearrange("(t p) d -> p t d", p=P))
+        w_rows = keep.tile([P, FEATURES], BF16)
+        nc.vector.memset(w_rows[:], 0.0)
+        nc.sync.dma_start(out=w_rows[0:VIEWS, :], in_=weight_tensor)
+        g_bf = keep.tile([P, TILES, TOKENS], BF16)
+        g_view = grad_out.rearrange("(t p) c -> p t c", p=P)
+        for g in range(PASSES):
+            rows = slice(g * PACK, (g + 1) * PACK)
+            nc.sync.dma_start(out=g_bf[:, rows, :], in_=g_view[:, rows, :])
+
+        sims = {}
+
+        def load_similarity(j):
+            sim_sb = sim_pool.tile([P, TOKENS], F32)
+            nc.sync.dma_start(out=sim_sb[:], in_=similarity[j * P : (j + 1) * P, :])
+            sims[j] = sim_sb
+
+        for j in range(SIM_AHEAD):
+            load_similarity(j)
+        w_all = keep.tile([P, COLUMNS], BF16)
+        nc.sync.dma_start(
+            out=w_all[:], in_=weight_tensor.rearrange("v d -> (v d)").partition_broadcast(P)
+        )
+
+        ident_bf = keep.tile([P, P], BF16)
+        make_identity(nc, ident_bf[:])
+        ident_f32 = keep.tile([P, P], F32)
+        make_identity(nc, ident_f32[:])
+
+        wT_ps = ps_half.tile([P, HALVES, P], BF16, tag="half")
+        for h in range(HALVES):
+            nc.tensor.transpose(wT_ps[:, h, :], w_rows[:, h * P : (h + 1) * P], ident_bf[:])
+        wT = keep.tile([P, HALVES, VIEWS], F32)
+        nc.vector.tensor_copy(out=wT[:], in_=wT_ps[:, :, 0:VIEWS])
+        w2T = keep.tile([P, HALVES, VIEWS], F32)
+        nc.vector.tensor_tensor(out=w2T[:], in0=wT[:], in1=wT[:], op=ALU.mult)
+        w_diag = keep.tile([P, HALVES, VIEWS, P], BF16)
+        for h in range(HALVES):
+            nc.vector.tensor_tensor(
+                out=w_diag[:, h, :, :],
+                in0=ident_bf[:].unsqueeze(1).to_broadcast([P, VIEWS, P]),
+                in1=wT[:, h, :].unsqueeze(2).to_broadcast([P, VIEWS, P]),
+                op=ALU.mult,
+            )
+        w2_rows = keep.tile([P, FEATURES], F32)
+        nc.vector.tensor_tensor(out=w2_rows[:], in0=w_rows[:], in1=w_rows[:], op=ALU.mult)
+
+        fT = keep.tile([P, HALVES, TILES, P], BF16)
+        norm = keep.tile([P, TILES * VIEWS], F32)
+        rn = keep.tile([P, TILES * VIEWS], F32)
+        rn8 = keep.tile([P, TILES * VIEWS], F32)
+        rn2 = keep.tile([P, TILES * VIEWS], F32)
+        for g in range(PASSES):
+            tiles = slice(g * PACK, (g + 1) * PACK)
+            fT_ps = ps_bank.tile([P, HALVES, PACK, P], BF16, tag="bank")
+            for h in range(HALVES):
+                for t in range(PACK):
+                    nc.tensor.transpose(
+                        fT_ps[:, h, t, :], f_bf[:, g * PACK + t, h * P : (h + 1) * P], ident_bf[:]
+                    )
+            nc.scalar.copy(out=fT[:, :, tiles, :], in_=fT_ps[:])
+            f2T = e_stage.tile([P, HALVES, PACK, P], F32, tag="sum4")
+            nc.vector.tensor_tensor(
+                out=f2T[:], in0=fT[:, :, tiles, :], in1=fT[:, :, tiles, :], op=ALU.mult
+            )
+            norm2 = ps_small.tile([P, PACK * VIEWS], F32, tag="small")
+            for t in range(PACK):
+                for h in range(HALVES):
+                    nc.tensor.matmul(
+                        out=norm2[:, t * VIEWS : (t + 1) * VIEWS],
+                        lhsT=f2T[:, h, t, :],
+                        rhs=w2T[:, h, :],
+                        start=(h == 0),
+                        stop=(h == HALVES - 1),
+                    )
+            cols = slice(g * PACK * VIEWS, (g + 1) * PACK * VIEWS)
+            nc.scalar.activation(out=norm[:, cols], in_=norm2[:], func=ACT.Sqrt)
+            nc.vector.tensor_scalar_max(out=norm[:, cols], in0=norm[:, cols], scalar1=EPS)
+            nc.vector.reciprocal(out=rn[:, cols], in_=norm[:, cols])
+            nc.vector.tensor_scalar_mul(out=rn8[:, cols], in0=rn[:, cols], scalar1=1.0 / VIEWS)
+            nc.vector.tensor_tensor(out=rn2[:, cols], in0=rn[:, cols], in1=rn[:, cols], op=ALU.mult)
+
+        c_codes = keep.tile([P, PASSES, COLUMNS], U32, align_bytes=64)
+        c_scales = keep.tile([P, PASSES, COLUMNS], U8, align_bytes=64)
+        h_codes = keep.tile([P, PASSES, TOKENS], U32, align_bytes=64)
+        h_scales = keep.tile([P, PASSES, TOKENS], U8, align_bytes=64)
+
+        def c_values(g, b, t, c_plain):
+            fw = ps_bank.tile([P, VIEWS_PER_BANK, HALVES, P], F32, tag="bank")
+            for h in range(HALVES):
+                nc.tensor.matmul(
+                    out=fw[:, :, h, :],
+                    lhsT=fT[:, h, g * PACK + t, :],
+                    rhs=w_diag[:, h, b * VIEWS_PER_BANK : (b + 1) * VIEWS_PER_BANK, :],
+                    start=True,
+                    stop=True,
+                )
+            for v in range(VIEWS_PER_BANK):
+                col = (g * PACK + t) * VIEWS + b * VIEWS_PER_BANK + v
+                nc.scalar.activation(
+                    out=c_plain[:, t, v * FEATURES : (v + 1) * FEATURES],
+                    in_=fw[:, v, :, :].rearrange("p h d -> p (h d)"),
+                    func=ACT.Copy,
+                    scale=rn[:, col : col + 1],
+                )
+
+        def h_transposes(j, g, gT):
+            gT_ps = ps_half.tile([P, PACK, P], BF16, tag="half")
+            simT_ps = ps_bank.tile([P, PACK, P], F32, tag="bank")
+            for t in range(PACK):
+                m_cols = slice((g * PACK + t) * P, (g * PACK + t + 1) * P)
+                nc.tensor.transpose(gT_ps[:, t, :], g_bf[:, j, m_cols], ident_bf[:])
+            for t in range(PACK):
+                m_cols = slice((g * PACK + t) * P, (g * PACK + t + 1) * P)
+                nc.tensor.transpose(simT_ps[:, t, :], sims[j][:, m_cols], ident_f32[:])
+            nc.scalar.copy(out=gT[:, g * PACK : (g + 1) * PACK, :], in_=gT_ps[:])
+            return simT_ps
+
+        h_grouped = keep.tile([P, PASSES, PACK * P, PACK], BF16, align_bytes=64)
+
+        for i in range(TILES):
+            g_c, b_c = divmod(i, BANKS)
+            if i + SIM_AHEAD < TILES:
+                load_similarity(i + SIM_AHEAD)
+            c_plain = c_stage.tile([P, PACK, BANK], BF16)
+            gT = h_stage.tile([P, TILES, P], BF16)
+            simT = []
+            for t in range(PACK):
+                c_values(g_c, b_c, t, c_plain)
+                if t < PASSES:
+                    simT.append(h_transposes(i, t, gT))
+            pair_sum = h_stage.tile([P, TILES, P], BF16)
+            nc.vector.tensor_tensor(
+                out=pair_sum[:], in0=g_bf[:, :, i * P : (i + 1) * P], in1=gT[:], op=ALU.add
+            )
+            c_grouped = c_stage.tile([P, BANK, PACK], BF16, align_bytes=64)
+            nc.vector.tensor_copy(
+                out=c_grouped[:].rearrange("p (c i) t -> p c t i", i=4),
+                in_=c_plain[:].rearrange("p t (c i) -> p c t i", i=4),
+            )
+            for g in range(PASSES):
+                nc.vector.scalar_tensor_tensor(
+                    out=h_grouped[:, g, (i % PACK) * P : (i % PACK + 1) * P, :],
+                    in0=simT[g][:].rearrange("p t n -> p n t"),
+                    scalar=THRESHOLD,
+                    in1=pair_sum[:, g * PACK : (g + 1) * PACK, :].rearrange("p t n -> p n t"),
+                    op0=ALU.is_gt,
+                    op1=ALU.mult,
+                )
+            cols = slice(b_c * BANK, (b_c + 1) * BANK)
+            nc.vector.quantize_mx(
+                out=c_codes[:, g_c, cols].bitcast(E4M3X4),
+                scales=c_scales[:, g_c, cols],
+                in_=c_grouped[:].rearrange("p c t -> p (c t)"),
+            )
+            if i % PACK == PACK - 1:
+                n_cols = slice((i - PACK + 1) * P, (i + 1) * P)
+                for g in range(PASSES):
+                    nc.vector.quantize_mx(
+                        out=h_codes[:, g, n_cols].bitcast(E5M2X4),
+                        scales=h_scales[:, g, n_cols],
+                        in_=h_grouped[:, g, :, :].rearrange("p n t -> p (n t)"),
+                    )
+
+        products = keep.tile([P, VIEWS, FEATURES], F32)
+        rho_pads = []
+        for i in range(2):
+            rho_pad = keep.tile([P, P], F32, name="rho_pad%d" % i)
+            nc.vector.memset(rho_pad[:], 0.0)
+            rho_pads.append(rho_pad)
+        dc, f_ps, scaled_w, terms, smalls, rhoTs, partial = {}, {}, {}, {}, {}, {}, {}
+
+        def multiply(j):
+            n_cols = slice(j * P, (j + 1) * P)
+            dc[j] = []
+            for b in range(BANKS):
+                cols = slice(b * BANK, (b + 1) * BANK)
+                bank = ps_bank.tile([P, BANK], F32, tag="bank", name="dc%d" % b)
+                for g in range(PASSES):
+                    nc.tensor.matmul_mx(
+                        out=bank[:],
+                        lhsT=h_codes[:, g, n_cols].bitcast(E5M2X4),
+                        lhsT_scale=h_scales[:, g, n_cols],
+                        rhs=c_codes[:, g, cols].bitcast(E4M3X4),
+                        rhs_scale=c_scales[:, g, cols],
+                        start=(g == 0),
+                        stop=(g == PASSES - 1),
+                    )
+                dc[j].append(bank)
+
+        def features_to_psum(j):
+            f_ps[j] = ps_half.tile([P, FEATURES], BF16, tag="half", name="f_ps")
+            for h in range(HALVES):
+                nc.tensor.transpose(f_ps[j][:, h * P : (h + 1) * P], fT[:, h, j, :], ident_bf[:])
+
+        def scale_weights(j):
+            scaled_w[j] = e_stage.tile([P, VIEWS, FEATURES], F32, name="scaled_w")
+            for v in range(VIEWS):
+                nc.scalar.activation(
+                    out=scaled_w[j][:, v, :],
+                    in_=w_all[:, v * FEATURES : (v + 1) * FEATURES],
+                    func=ACT.Copy,
+                    scale=rn8[:, j * VIEWS + v : j * VIEWS + v + 1],
+                )
+
+        def weigh(j):
+            terms[j] = e_stage.tile([P, VIEWS, FEATURES], F32, name="terms")
+            for b in range(BANKS):
+                views = slice(b * VIEWS_PER_BANK, (b + 1) * VIEWS_PER_BANK)
+                nc.vector.tensor_tensor(
+                    out=terms[j][:, views, :].rearrange("p v d -> p (v d)"),
+                    in0=dc[j][b][:],
+                    in1=scaled_w[j][:, views, :].rearrange("p v d -> p (v d)"),
+                    op=ALU.mult,
+                )
+
+        def project(j):
+            r = e_stage.tile([P, VIEWS], F32)
+            for v in range(VIEWS):
+                nc.vector.scalar_tensor_tensor(
+                    out=products[:, v, :],
+                    in0=f_ps[j][:],
+                    scalar=1.0,
+                    in1=terms[j][:, v, :],
+                    op0=ALU.mult,
+                    op1=ALU.mult,
+                    accum_out=r[:, v : v + 1],
+                )
+            nc.vector.tensor_tensor(
+                out=rho_pads[j % 2][:, 0:VIEWS],
+                in0=r[:],
+                in1=rn2[:, j * VIEWS : (j + 1) * VIEWS],
+                op=ALU.mult,
+            )
+
+        def rho_transpose(j):
+            smalls[j] = ps_small.tile([P, P + FEATURES], F32, tag="small", name="small")
+            nc.tensor.transpose(smalls[j][:, 0:P], rho_pads[j % 2][:], ident_f32[:])
+            rhoTs[j] = e_stage.tile([P, P], F32, name="rhoT")
+            nc.scalar.copy(out=rhoTs[j][:], in_=smalls[j][:, 0:P])
+
+        def rho_times_w2(j):
+            nc.tensor.matmul(
+                out=smalls[j][:, P:], lhsT=rhoTs[j][:], rhs=w2_rows[:], start=True, stop=True
+            )
+
+        def add_views(j):
+            sum4 = e_stage.tile([P, 4, FEATURES], F32)
+            nc.gpsimd.tensor_tensor(
+                out=sum4[:], in0=terms[j][:, 0:4, :], in1=terms[j][:, 4:8, :], op=ALU.add
+            )
+            sum2 = e_stage.tile([P, 2, FEATURES], F32)
+            nc.gpsimd.tensor_tensor(out=sum2[:], in0=sum4[:, 0:2, :], in1=sum4[:, 2:4, :], op=ALU.add)
+            partial[j] = e_stage.tile([P, FEATURES], F32, name="partial")
+            nc.gpsimd.tensor_tensor(out=partial[j][:], in0=sum2[:, 0, :], in1=sum2[:, 1, :], op=ALU.add)
+
+        def subtract_and_store(j):
+            correction = e_stage.tile([P, FEATURES], F32)
+            nc.vector.scalar_tensor_tensor(
+                out=correction[:],
+                in0=smalls[j][:, P:],
+                scalar=-1.0,
+                in1=f_bf[:, j, :],
+                op0=ALU.mult,
+                op1=ALU.mult,
+            )
+            result = e_stage.tile([P, FEATURES], F32)
+            nc.gpsimd.tensor_tensor(out=result[:], in0=partial[j][:], in1=correction[:], op=ALU.add)
+            nc.sync.dma_start(out=out[j * P : (j + 1) * P, :], in_=result[:])
+
+        scale_weights(0)
+        multiply(0)
+        for j in range(TILES):
+            if j + 1 < TILES:
+                scale_weights(j + 1)
+            if j > 0:
+                rho_transpose(j - 1)
+            features_to_psum(j)
+            if j > 0:
+                rho_times_w2(j - 1)
+            if j + 1 < TILES:
+                multiply(j + 1)
+            weigh(j)
+            if j > 0:
+                subtract_and_store(j - 1)
+            add_views(j)
+            project(j)
+        rho_transpose(TILES - 1)
+        rho_times_w2(TILES - 1)
+        subtract_and_store(TILES - 1)

@@ -39,8 +39,9 @@ def tile_graphlearner_v_kernel(tc, features, weight_tensor, similarity, grad_out
         sim_pool = stack.enter_context(tc.tile_pool(name="sim_pool", bufs=SIM_AHEAD))
         h_stage = stack.enter_context(tc.tile_pool(name="h_stage", bufs=2))
         e_stage = stack.enter_context(tc.tile_pool(name="e_stage", bufs=2))
-        ps_bank = stack.enter_context(tc.psum_pool(name="ps_bank", bufs=5))
-        ps_half = stack.enter_context(tc.psum_pool(name="ps_half", bufs=2))
+        t_stage = stack.enter_context(tc.tile_pool(name="t_stage", bufs=3))
+        ps_bank = stack.enter_context(tc.psum_pool(name="ps_bank", bufs=4))
+        ps_turn = stack.enter_context(tc.psum_pool(name="ps_turn", bufs=3))
         ps_small = stack.enter_context(tc.psum_pool(name="ps_small", bufs=1))
 
         warm = keep.tile([P, 1], F32)
@@ -58,15 +59,22 @@ def tile_graphlearner_v_kernel(tc, features, weight_tensor, similarity, grad_out
             rows = slice(g * PACK, (g + 1) * PACK)
             nc.sync.dma_start(out=g_bf[:, rows, :], in_=g_view[:, rows, :])
 
+        blocks = [(G, C) for C in range(PASSES) for G in range(PASSES)]
         sims = {}
 
-        def load_similarity(j):
-            sim_sb = sim_pool.tile([P, TOKENS], F32)
-            nc.sync.dma_start(out=sim_sb[:], in_=similarity[j * P : (j + 1) * P, :])
-            sims[j] = sim_sb
+        def load_similarity(u):
+            G, C = blocks[u]
+            sim_sb = sim_pool.tile([P, PACK, BANK], F32)
+            nc.sync.dma_start(
+                out=sim_sb[:],
+                in_=similarity[G * BANK : (G + 1) * BANK, C * BANK : (C + 1) * BANK].rearrange(
+                    "(t p) n -> p t n", p=P
+                ),
+            )
+            sims[u] = sim_sb
 
-        for j in range(SIM_AHEAD):
-            load_similarity(j)
+        for u in range(SIM_AHEAD):
+            load_similarity(u)
         w_all = keep.tile([P, COLUMNS], BF16)
         nc.sync.dma_start(
             out=w_all[:], in_=weight_tensor.rearrange("v d -> (v d)").partition_broadcast(P)
@@ -77,7 +85,7 @@ def tile_graphlearner_v_kernel(tc, features, weight_tensor, similarity, grad_out
         ident_f32 = keep.tile([P, P], F32)
         make_identity(nc, ident_f32[:])
 
-        wT_ps = ps_half.tile([P, HALVES, P], BF16, tag="half")
+        wT_ps = ps_turn.tile([P, HALVES, P], BF16, tag="turn")
         for h in range(HALVES):
             nc.tensor.transpose(wT_ps[:, h, :], w_rows[:, h * P : (h + 1) * P], ident_bf[:])
         wT = keep.tile([P, HALVES, VIEWS], F32)
@@ -154,63 +162,92 @@ def tile_graphlearner_v_kernel(tc, features, weight_tensor, similarity, grad_out
                     scale=rn[:, col : col + 1],
                 )
 
-        def h_transposes(j, g, gT):
-            gT_ps = ps_half.tile([P, PACK, P], BF16, tag="half")
-            simT_ps = ps_bank.tile([P, PACK, P], F32, tag="bank")
-            for t in range(PACK):
-                m_cols = slice((g * PACK + t) * P, (g * PACK + t + 1) * P)
-                nc.tensor.transpose(gT_ps[:, t, :], g_bf[:, j, m_cols], ident_bf[:])
-            for t in range(PACK):
-                m_cols = slice((g * PACK + t) * P, (g * PACK + t + 1) * P)
-                nc.tensor.transpose(simT_ps[:, t, :], sims[j][:, m_cols], ident_f32[:])
-            nc.scalar.copy(out=gT[:, g * PACK : (g + 1) * PACK, :], in_=gT_ps[:])
-            return simT_ps
+        c_plains, c_groupeds, gTs, pair_sums, h_groupeds = {}, {}, {}, {}, {}
 
-        h_grouped = keep.tile([P, PASSES, PACK * P, PACK], BF16, align_bytes=64)
-
-        for i in range(TILES):
+        def c_produce(i):
             g_c, b_c = divmod(i, BANKS)
-            if i + SIM_AHEAD < TILES:
-                load_similarity(i + SIM_AHEAD)
-            c_plain = c_stage.tile([P, PACK, BANK], BF16)
-            gT = h_stage.tile([P, TILES, P], BF16)
-            simT = []
+            c_plains[i] = c_stage.tile([P, PACK, BANK], BF16, name="c_plain")
             for t in range(PACK):
-                c_values(g_c, b_c, t, c_plain)
-                if t < PASSES:
-                    simT.append(h_transposes(i, t, gT))
-            pair_sum = h_stage.tile([P, TILES, P], BF16)
-            nc.vector.tensor_tensor(
-                out=pair_sum[:], in0=g_bf[:, :, i * P : (i + 1) * P], in1=gT[:], op=ALU.add
-            )
-            c_grouped = c_stage.tile([P, BANK, PACK], BF16, align_bytes=64)
+                c_values(g_c, b_c, t, c_plains[i])
+
+        def c_group(i):
+            c_groupeds[i] = c_stage.tile([P, BANK, PACK], BF16, align_bytes=64, name="c_grouped")
             nc.vector.tensor_copy(
-                out=c_grouped[:].rearrange("p (c i) t -> p c t i", i=4),
-                in_=c_plain[:].rearrange("p t (c i) -> p c t i", i=4),
+                out=c_groupeds[i][:].rearrange("p (c i) t -> p c t i", i=4),
+                in_=c_plains[i][:].rearrange("p t (c i) -> p c t i", i=4),
             )
-            for g in range(PASSES):
-                nc.vector.scalar_tensor_tensor(
-                    out=h_grouped[:, g, (i % PACK) * P : (i % PACK + 1) * P, :],
-                    in0=simT[g][:].rearrange("p t n -> p n t"),
-                    scalar=THRESHOLD,
-                    in1=pair_sum[:, g * PACK : (g + 1) * PACK, :].rearrange("p t n -> p n t"),
-                    op0=ALU.is_gt,
-                    op1=ALU.mult,
-                )
+
+        def c_quantise(i):
+            g_c, b_c = divmod(i, BANKS)
             cols = slice(b_c * BANK, (b_c + 1) * BANK)
             nc.vector.quantize_mx(
                 out=c_codes[:, g_c, cols].bitcast(E4M3X4),
                 scales=c_scales[:, g_c, cols],
-                in_=c_grouped[:].rearrange("p c t -> p (c t)"),
+                in_=c_groupeds[i][:].rearrange("p c t -> p (c t)"),
             )
-            if i % PACK == PACK - 1:
-                n_cols = slice((i - PACK + 1) * P, (i + 1) * P)
-                for g in range(PASSES):
-                    nc.vector.quantize_mx(
-                        out=h_codes[:, g, n_cols].bitcast(E5M2X4),
-                        scales=h_scales[:, g, n_cols],
-                        in_=h_grouped[:, g, :, :].rearrange("p n t -> p (n t)"),
-                    )
+
+        def h_transposes(u):
+            G, C = blocks[u]
+            gTs[u] = []
+            for half in range(2):
+                gT_ps = ps_turn.tile([P, 2, PACK, P], BF16, tag="turn", name="gT_ps")
+                for t2 in range(2):
+                    m0 = (G * PACK + half * 2 + t2) * P
+                    for jn in range(PACK):
+                        nc.tensor.transpose(
+                            gT_ps[:, t2, jn, :], g_bf[:, C * PACK + jn, m0 : m0 + P], ident_bf[:]
+                        )
+                gTs[u].append(gT_ps)
+
+        def h_sum(u):
+            G, C = blocks[u]
+            pair_sums[u] = h_stage.tile([P, PACK, BANK], BF16, name="pair_sum")
+            for half in range(2):
+                nc.vector.tensor_tensor(
+                    out=pair_sums[u][:, half * 2 : half * 2 + 2, :],
+                    in0=g_bf[:, G * PACK + half * 2 : G * PACK + half * 2 + 2, C * BANK : (C + 1) * BANK],
+                    in1=gTs[u][half][:].rearrange("p t j n -> p t (j n)"),
+                    op=ALU.add,
+                )
+
+        def h_mask(u):
+            h_groupeds[u] = h_stage.tile([P, BANK, PACK], BF16, align_bytes=64, name="h_grouped")
+            nc.vector.scalar_tensor_tensor(
+                out=h_groupeds[u][:],
+                in0=sims[u][:].rearrange("p t n -> p n t"),
+                scalar=THRESHOLD,
+                in1=pair_sums[u][:].rearrange("p t n -> p n t"),
+                op0=ALU.is_gt,
+                op1=ALU.mult,
+            )
+            if u + SIM_AHEAD < len(blocks):
+                load_similarity(u + SIM_AHEAD)
+
+        def h_quantise(u):
+            G, C = blocks[u]
+            n_cols = slice(C * BANK, (C + 1) * BANK)
+            nc.vector.quantize_mx(
+                out=h_codes[:, G, n_cols].bitcast(E5M2X4),
+                scales=h_scales[:, G, n_cols],
+                in_=h_groupeds[u][:].rearrange("p n t -> p (n t)"),
+            )
+
+        h_at_step = {3: 0, 5: 1, 7: 2, 9: 3}
+        c_produce(0)
+        for i in range(TILES):
+            if i + 1 < TILES:
+                c_produce(i + 1)
+            if i + 1 in h_at_step:
+                h_transposes(h_at_step[i + 1])
+            u = h_at_step.get(i)
+            if u is not None:
+                h_sum(u)
+            c_group(i)
+            if u is not None:
+                h_mask(u)
+            c_quantise(i)
+            if u is not None:
+                h_quantise(u)
 
         products = keep.tile([P, VIEWS, FEATURES], F32)
         rho_pads = []
@@ -218,12 +255,11 @@ def tile_graphlearner_v_kernel(tc, features, weight_tensor, similarity, grad_out
             rho_pad = keep.tile([P, P], F32, name="rho_pad%d" % i)
             nc.vector.memset(rho_pad[:], 0.0)
             rho_pads.append(rho_pad)
-        dc, f_ps, scaled_w, terms, smalls, rhoTs, partial = {}, {}, {}, {}, {}, {}, {}
+        dc, scaled_w, terms, smalls, rhoTs, corrections, outT_pss, outTs = {}, {}, {}, {}, {}, {}, {}, {}
 
-        def multiply(j):
+        def multiply(j, banks):
             n_cols = slice(j * P, (j + 1) * P)
-            dc[j] = []
-            for b in range(BANKS):
+            for b in banks:
                 cols = slice(b * BANK, (b + 1) * BANK)
                 bank = ps_bank.tile([P, BANK], F32, tag="bank", name="dc%d" % b)
                 for g in range(PASSES):
@@ -236,12 +272,7 @@ def tile_graphlearner_v_kernel(tc, features, weight_tensor, similarity, grad_out
                         start=(g == 0),
                         stop=(g == PASSES - 1),
                     )
-                dc[j].append(bank)
-
-        def features_to_psum(j):
-            f_ps[j] = ps_half.tile([P, FEATURES], BF16, tag="half", name="f_ps")
-            for h in range(HALVES):
-                nc.tensor.transpose(f_ps[j][:, h * P : (h + 1) * P], fT[:, h, j, :], ident_bf[:])
+                dc[j, b] = bank
 
         def scale_weights(j):
             scaled_w[j] = e_stage.tile([P, VIEWS, FEATURES], F32, name="scaled_w")
@@ -254,12 +285,12 @@ def tile_graphlearner_v_kernel(tc, features, weight_tensor, similarity, grad_out
                 )
 
         def weigh(j):
-            terms[j] = e_stage.tile([P, VIEWS, FEATURES], F32, name="terms")
+            terms[j] = t_stage.tile([P, VIEWS, FEATURES], F32, name="terms")
             for b in range(BANKS):
                 views = slice(b * VIEWS_PER_BANK, (b + 1) * VIEWS_PER_BANK)
                 nc.vector.tensor_tensor(
                     out=terms[j][:, views, :].rearrange("p v d -> p (v d)"),
-                    in0=dc[j][b][:],
+                    in0=dc[j, b][:],
                     in1=scaled_w[j][:, views, :].rearrange("p v d -> p (v d)"),
                     op=ALU.mult,
                 )
@@ -269,7 +300,7 @@ def tile_graphlearner_v_kernel(tc, features, weight_tensor, similarity, grad_out
             for v in range(VIEWS):
                 nc.vector.scalar_tensor_tensor(
                     out=products[:, v, :],
-                    in0=f_ps[j][:],
+                    in0=f_bf[:, j, :],
                     scalar=1.0,
                     in1=terms[j][:, v, :],
                     op0=ALU.mult,
@@ -294,47 +325,80 @@ def tile_graphlearner_v_kernel(tc, features, weight_tensor, similarity, grad_out
                 out=smalls[j][:, P:], lhsT=rhoTs[j][:], rhs=w2_rows[:], start=True, stop=True
             )
 
-        def add_views(j):
-            sum4 = e_stage.tile([P, 4, FEATURES], F32)
-            nc.gpsimd.tensor_tensor(
-                out=sum4[:], in0=terms[j][:, 0:4, :], in1=terms[j][:, 4:8, :], op=ALU.add
-            )
-            sum2 = e_stage.tile([P, 2, FEATURES], F32)
-            nc.gpsimd.tensor_tensor(out=sum2[:], in0=sum4[:, 0:2, :], in1=sum4[:, 2:4, :], op=ALU.add)
-            partial[j] = e_stage.tile([P, FEATURES], F32, name="partial")
-            nc.gpsimd.tensor_tensor(out=partial[j][:], in0=sum2[:, 0, :], in1=sum2[:, 1, :], op=ALU.add)
-
-        def subtract_and_store(j):
-            correction = e_stage.tile([P, FEATURES], F32)
+        def correct(j):
+            corrections[j] = e_stage.tile([P, FEATURES], F32, name="correction")
             nc.vector.scalar_tensor_tensor(
-                out=correction[:],
+                out=corrections[j][:],
                 in0=smalls[j][:, P:],
                 scalar=-1.0,
                 in1=f_bf[:, j, :],
                 op0=ALU.mult,
                 op1=ALU.mult,
             )
+
+        def add_views(j, h):
+            if h == 0:
+                outT_pss[j] = ps_turn.tile([P, HALVES, P], F32, tag="turn", name="outT_ps")
+            d_cols = slice(h * P, (h + 1) * P)
+            for v in range(VIEWS):
+                nc.tensor.matmul(
+                    out=outT_pss[j][:, h, :],
+                    lhsT=terms[j][:, v, d_cols],
+                    rhs=ident_f32[:],
+                    is_transpose=True,
+                    start=(v == 0),
+                    stop=False,
+                )
+            nc.tensor.matmul(
+                out=outT_pss[j][:, h, :],
+                lhsT=corrections[j][:, d_cols],
+                rhs=ident_f32[:],
+                is_transpose=True,
+                start=False,
+                stop=True,
+            )
+            if h == HALVES - 1:
+                outTs[j] = e_stage.tile([P, HALVES, P], F32, name="outT")
+                nc.scalar.copy(out=outTs[j][:], in_=outT_pss[j][:])
+
+        def turn_back_and_store(j):
+            out_ps = ps_turn.tile([P, FEATURES], F32, tag="turn", name="out_ps")
+            for h in range(HALVES):
+                nc.tensor.transpose(out_ps[:, h * P : (h + 1) * P], outTs[j][:, h, :], ident_f32[:])
             result = e_stage.tile([P, FEATURES], F32)
-            nc.gpsimd.tensor_tensor(out=result[:], in0=partial[j][:], in1=correction[:], op=ALU.add)
+            nc.scalar.copy(out=result[:], in_=out_ps[:])
             nc.sync.dma_start(out=out[j * P : (j + 1) * P, :], in_=result[:])
 
+        h_at_tile = {0: 4, 1: 5, 3: 6, 4: 7, 5: 8}
         scale_weights(0)
-        multiply(0)
-        for j in range(TILES):
+        multiply(0, range(BANKS))
+        h_transposes(h_at_tile[0])
+        for j in range(TILES + 2):
             if j + 1 < TILES:
                 scale_weights(j + 1)
-            if j > 0:
+            if 0 < j <= TILES:
                 rho_transpose(j - 1)
-            features_to_psum(j)
-            if j > 0:
+            if j > 1:
+                add_views(j - 2, 0)
+            if 0 < j <= TILES:
                 rho_times_w2(j - 1)
+            if j > 1:
+                add_views(j - 2, 1)
             if j + 1 < TILES:
-                multiply(j + 1)
-            weigh(j)
-            if j > 0:
-                subtract_and_store(j - 1)
-            add_views(j)
-            project(j)
-        rho_transpose(TILES - 1)
-        rho_times_w2(TILES - 1)
-        subtract_and_store(TILES - 1)
+                multiply(j + 1, range(BANKS))
+            if j > 1:
+                turn_back_and_store(j - 2)
+            if j + 1 in h_at_tile:
+                h_transposes(h_at_tile[j + 1])
+            if j < TILES:
+                weigh(j)
+            if j - 1 in h_at_tile:
+                h_quantise(h_at_tile[j - 1])
+            if 0 < j <= TILES:
+                correct(j - 1)
+            if j in h_at_tile:
+                h_sum(h_at_tile[j])
+            if j < TILES:
+                project(j)
+            if j in h_at_tile:
+                h_mask(h_at_tile[j])

@@ -39,7 +39,7 @@ def tile_graphlearner_v_kernel(tc, features, weight_tensor, similarity, grad_out
         sim_pool = stack.enter_context(tc.tile_pool(name="sim_pool", bufs=SIM_AHEAD))
         h_stage = stack.enter_context(tc.tile_pool(name="h_stage", bufs=2))
         e_stage = stack.enter_context(tc.tile_pool(name="e_stage", bufs=2))
-        t_stage = stack.enter_context(tc.tile_pool(name="t_stage", bufs=3))
+        t_stage = stack.enter_context(tc.tile_pool(name="t_stage", bufs=4))
         ps_bank = stack.enter_context(tc.psum_pool(name="ps_bank", bufs=4))
         ps_turn = stack.enter_context(tc.psum_pool(name="ps_turn", bufs=3))
         ps_small = stack.enter_context(tc.psum_pool(name="ps_small", bufs=1))
@@ -117,7 +117,7 @@ def tile_graphlearner_v_kernel(tc, features, weight_tensor, similarity, grad_out
                         fT_ps[:, h, t, :], f_bf[:, g * PACK + t, h * P : (h + 1) * P], ident_bf[:]
                     )
             nc.scalar.copy(out=fT[:, :, tiles, :], in_=fT_ps[:])
-            f2T = e_stage.tile([P, HALVES, PACK, P], F32, tag="sum4")
+            f2T = e_stage.tile([P, HALVES, PACK, P], F32, tag="scaled_w")
             nc.vector.tensor_tensor(
                 out=f2T[:], in0=fT[:, :, tiles, :], in1=fT[:, :, tiles, :], op=ALU.mult
             )
@@ -232,7 +232,7 @@ def tile_graphlearner_v_kernel(tc, features, weight_tensor, similarity, grad_out
                 in_=h_groupeds[u][:].rearrange("p n t -> p (n t)"),
             )
 
-        h_at_step = {3: 0, 5: 1, 7: 2, 9: 3}
+        h_at_step = {3: 0, 6: 1, 9: 2}
         c_produce(0)
         for i in range(TILES):
             if i + 1 < TILES:
@@ -249,13 +249,12 @@ def tile_graphlearner_v_kernel(tc, features, weight_tensor, similarity, grad_out
             if u is not None:
                 h_quantise(u)
 
-        products = keep.tile([P, VIEWS, FEATURES], F32)
         rho_pads = []
         for i in range(2):
             rho_pad = keep.tile([P, P], F32, name="rho_pad%d" % i)
             nc.vector.memset(rho_pad[:], 0.0)
             rho_pads.append(rho_pad)
-        dc, scaled_w, terms, smalls, rhoTs, corrections, outT_pss, outTs = {}, {}, {}, {}, {}, {}, {}, {}
+        dc, scaled_w, terms, prods, smalls, rhoTs, corrections, outT_pss, outTs = {}, {}, {}, {}, {}, {}, {}, {}, {}
 
         def multiply(j, banks):
             n_cols = slice(j * P, (j + 1) * P)
@@ -295,24 +294,28 @@ def tile_graphlearner_v_kernel(tc, features, weight_tensor, similarity, grad_out
                     op=ALU.mult,
                 )
 
-        def project(j):
-            r = e_stage.tile([P, VIEWS], F32)
-            for v in range(VIEWS):
-                nc.vector.scalar_tensor_tensor(
-                    out=products[:, v, :],
-                    in0=f_bf[:, j, :],
-                    scalar=1.0,
-                    in1=terms[j][:, v, :],
-                    op0=ALU.mult,
-                    op1=ALU.mult,
-                    accum_out=r[:, v : v + 1],
+        def product(j):
+            lo = c_stage.tile([P, VIEWS // 2, FEATURES], F32, tag="c_plain", name="prod_lo")
+            hi = c_stage.tile([P, VIEWS // 2, FEATURES], F32, tag="c_grouped", name="prod_hi", align_bytes=64)
+            prods[j] = (lo, hi)
+            for b in range(BANKS):
+                nc.gpsimd.tensor_tensor(
+                    out=prods[j][b // 2][:, 2 * (b % 2) : 2 * (b % 2) + 2, :],
+                    in0=terms[j][:, 2 * b : 2 * b + 2, :],
+                    in1=f_bf[:, j, :].unsqueeze(1).to_broadcast([P, 2, FEATURES]),
+                    op=ALU.mult,
                 )
-            nc.vector.tensor_tensor(
-                out=rho_pads[j % 2][:, 0:VIEWS],
-                in0=r[:],
-                in1=rn2[:, j * VIEWS : (j + 1) * VIEWS],
-                op=ALU.mult,
-            )
+
+        def accumulate(j):
+            unread = e_stage.tile([P, FEATURES], BF16, name="unread")
+            for v in range(VIEWS):
+                nc.scalar.activation(
+                    out=unread[:],
+                    in_=prods[j][v // 4][:, v % 4, :],
+                    func=ACT.Copy,
+                    scale=rn2[:, j * VIEWS + v : j * VIEWS + v + 1],
+                    accum_out=rho_pads[j % 2][:, v : v + 1],
+                )
 
         def rho_transpose(j):
             smalls[j] = ps_small.tile([P, P + FEATURES], F32, tag="small", name="small")
@@ -369,36 +372,37 @@ def tile_graphlearner_v_kernel(tc, features, weight_tensor, similarity, grad_out
             nc.scalar.copy(out=result[:], in_=out_ps[:])
             nc.sync.dma_start(out=out[j * P : (j + 1) * P, :], in_=result[:])
 
-        h_at_tile = {0: 4, 1: 5, 3: 6, 4: 7, 5: 8}
+        h_at_tile = {0: 3, 1: 4, 2: 5, 4: 6, 5: 7, 6: 8}
         scale_weights(0)
         multiply(0, range(BANKS))
         h_transposes(h_at_tile[0])
-        for j in range(TILES + 2):
+        for j in range(TILES + 3):
             if j + 1 < TILES:
                 scale_weights(j + 1)
-            if 0 < j <= TILES:
-                rho_transpose(j - 1)
-            if j > 1:
-                add_views(j - 2, 0)
-            if 0 < j <= TILES:
-                rho_times_w2(j - 1)
-            if j > 1:
-                add_views(j - 2, 1)
+            if 2 <= j < TILES + 2:
+                rho_transpose(j - 2)
+            if j >= 3:
+                add_views(j - 3, 0)
+            if 2 <= j < TILES + 2:
+                rho_times_w2(j - 2)
+            if j >= 3:
+                add_views(j - 3, 1)
             if j + 1 < TILES:
                 multiply(j + 1, range(BANKS))
-            if j > 1:
-                turn_back_and_store(j - 2)
+            if j >= 3:
+                turn_back_and_store(j - 3)
             if j + 1 in h_at_tile:
                 h_transposes(h_at_tile[j + 1])
-            if j < TILES:
-                weigh(j)
-            if j - 1 in h_at_tile:
-                h_quantise(h_at_tile[j - 1])
-            if 0 < j <= TILES:
-                correct(j - 1)
             if j in h_at_tile:
                 h_sum(h_at_tile[j])
             if j < TILES:
-                project(j)
+                weigh(j)
+                product(j)
             if j in h_at_tile:
                 h_mask(h_at_tile[j])
+            if 2 <= j < TILES + 2:
+                correct(j - 2)
+            if 1 <= j < TILES + 1:
+                accumulate(j - 1)
+            if j in h_at_tile:
+                h_quantise(h_at_tile[j])

@@ -60,10 +60,11 @@ def tile_graphlearner_v_kernel(tc, features, weight_tensor, similarity, grad_out
             nc.sync.dma_start(out=g_bf[:, rows, :], in_=g_view[:, rows, :])
 
         blocks = [(G, C) for C in range(PASSES) for G in range(PASSES)]
+        direct = [u for u in range(len(blocks)) if blocks[u][0] >= blocks[u][1]]
         sims = {}
 
-        def load_similarity(u):
-            G, C = blocks[u]
+        def load_similarity(k):
+            G, C = blocks[direct[k]]
             sim_sb = sim_pool.tile([P, PACK, BANK], F32)
             nc.sync.dma_start(
                 out=sim_sb[:],
@@ -71,10 +72,10 @@ def tile_graphlearner_v_kernel(tc, features, weight_tensor, similarity, grad_out
                     "(t p) n -> p t n", p=P
                 ),
             )
-            sims[u] = sim_sb
+            sims[direct[k]] = sim_sb
 
-        for u in range(SIM_AHEAD):
-            load_similarity(u)
+        for k in range(SIM_AHEAD):
+            load_similarity(k)
         w_all = keep.tile([P, COLUMNS], BF16)
         nc.sync.dma_start(
             out=w_all[:], in_=weight_tensor.rearrange("v d -> (v d)").partition_broadcast(P)
@@ -211,7 +212,10 @@ def tile_graphlearner_v_kernel(tc, features, weight_tensor, similarity, grad_out
                 )
 
         def h_mask(u):
-            h_groupeds[u] = h_stage.tile([P, BANK, PACK], BF16, align_bytes=64, name="h_grouped")
+            if blocks[u][0] > blocks[u][1]:
+                h_groupeds[u] = keep.tile([P, BANK, PACK], BF16, align_bytes=64, name="h_kept%d" % u)
+            else:
+                h_groupeds[u] = h_stage.tile([P, BANK, PACK], BF16, align_bytes=64, name="h_grouped")
             nc.vector.scalar_tensor_tensor(
                 out=h_groupeds[u][:],
                 in0=sims[u][:].rearrange("p t n -> p n t"),
@@ -220,8 +224,29 @@ def tile_graphlearner_v_kernel(tc, features, weight_tensor, similarity, grad_out
                 op0=ALU.is_gt,
                 op1=ALU.mult,
             )
-            if u + SIM_AHEAD < len(blocks):
-                load_similarity(u + SIM_AHEAD)
+            if direct.index(u) + SIM_AHEAD < len(direct):
+                load_similarity(direct.index(u) + SIM_AHEAD)
+
+        def h_mirror_transposes(u):
+            G, C = blocks[u]
+            source = h_groupeds[blocks.index((C, G))]
+            gTs[u] = []
+            for half in range(2):
+                hT_ps = ps_turn.tile([P, PACK, 2, P], BF16, tag="turn", name="hT_ps")
+                for t2 in range(PACK):
+                    for t in range(2):
+                        nc.tensor.transpose(
+                            hT_ps[:, t2, t, :], source[:, t2 * P : (t2 + 1) * P, half * 2 + t], ident_bf[:]
+                        )
+                gTs[u].append(hT_ps)
+
+        def h_mirror_copy(u):
+            h_groupeds[u] = h_stage.tile([P, BANK, PACK], BF16, align_bytes=64, name="h_grouped")
+            for half in range(2):
+                nc.scalar.copy(
+                    out=h_groupeds[u][:, half * 2 * P : (half + 1) * 2 * P, :],
+                    in_=gTs[u][half][:].rearrange("p m t n -> p (t n) m"),
+                )
 
         def h_quantise(u):
             G, C = blocks[u]
@@ -254,7 +279,8 @@ def tile_graphlearner_v_kernel(tc, features, weight_tensor, similarity, grad_out
             rho_pad = keep.tile([P, P], F32, name="rho_pad%d" % i)
             nc.vector.memset(rho_pad[:], 0.0)
             rho_pads.append(rho_pad)
-        dc, scaled_w, terms, prods, smalls, rhoTs, corrections, outT_pss, outTs = {}, {}, {}, {}, {}, {}, {}, {}, {}
+        view_sums = {}
+        dc, terms, prods, smalls, rhoTs, corrections, outT_pss, outTs = {}, {}, {}, {}, {}, {}, {}, {}
 
         def multiply(j, banks):
             n_cols = slice(j * P, (j + 1) * P)
@@ -273,25 +299,17 @@ def tile_graphlearner_v_kernel(tc, features, weight_tensor, similarity, grad_out
                     )
                 dc[j, b] = bank
 
-        def scale_weights(j):
-            scaled_w[j] = e_stage.tile([P, VIEWS, FEATURES], F32, name="scaled_w")
-            for v in range(VIEWS):
-                nc.scalar.activation(
-                    out=scaled_w[j][:, v, :],
-                    in_=w_all[:, v * FEATURES : (v + 1) * FEATURES],
-                    func=ACT.Copy,
-                    scale=rn8[:, j * VIEWS + v : j * VIEWS + v + 1],
-                )
-
         def weigh(j):
             terms[j] = t_stage.tile([P, VIEWS, FEATURES], F32, name="terms")
-            for b in range(BANKS):
-                views = slice(b * VIEWS_PER_BANK, (b + 1) * VIEWS_PER_BANK)
-                nc.vector.tensor_tensor(
-                    out=terms[j][:, views, :].rearrange("p v d -> p (v d)"),
-                    in0=dc[j, b][:],
-                    in1=scaled_w[j][:, views, :].rearrange("p v d -> p (v d)"),
-                    op=ALU.mult,
+            for v in range(VIEWS):
+                b, half = divmod(v, VIEWS_PER_BANK)
+                nc.vector.scalar_tensor_tensor(
+                    out=terms[j][:, v, :],
+                    in0=dc[j, b][:, half * FEATURES : (half + 1) * FEATURES],
+                    scalar=rn8[:, j * VIEWS + v : j * VIEWS + v + 1],
+                    in1=w_all[:, v * FEATURES : (v + 1) * FEATURES],
+                    op0=ALU.mult,
+                    op1=ALU.mult,
                 )
 
         def product(j):
@@ -339,6 +357,19 @@ def tile_graphlearner_v_kernel(tc, features, weight_tensor, similarity, grad_out
                 op1=ALU.mult,
             )
 
+        def finish_last(j):
+            result = e_stage.tile([P, FEATURES], F32, name="result")
+            nc.vector.tensor_tensor(out=result[:], in0=view_sums[j][:], in1=corrections[j][:], op=ALU.add)
+            nc.sync.dma_start(out=out[j * P : (j + 1) * P, :], in_=result[:])
+
+        def sum_views(j):
+            sum4 = e_stage.tile([P, 4, FEATURES], F32, tag="scaled_w", name="sum4")
+            nc.vector.tensor_tensor(out=sum4[:], in0=terms[j][:, 0:4, :], in1=terms[j][:, 4:8, :], op=ALU.add)
+            sum2 = e_stage.tile([P, 2, FEATURES], F32, name="sum2")
+            nc.vector.tensor_tensor(out=sum2[:], in0=sum4[:, 0:2, :], in1=sum4[:, 2:4, :], op=ALU.add)
+            view_sums[j] = e_stage.tile([P, FEATURES], F32, name="view_sum")
+            nc.vector.tensor_tensor(out=view_sums[j][:], in0=sum2[:, 0, :], in1=sum2[:, 1, :], op=ALU.add)
+
         def add_views(j, h):
             if h == 0:
                 outT_pss[j] = ps_turn.tile([P, HALVES, P], F32, tag="turn", name="outT_ps")
@@ -368,40 +399,48 @@ def tile_graphlearner_v_kernel(tc, features, weight_tensor, similarity, grad_out
             out_ps = ps_turn.tile([P, FEATURES], F32, tag="turn", name="out_ps")
             for h in range(HALVES):
                 nc.tensor.transpose(out_ps[:, h * P : (h + 1) * P], outTs[j][:, h, :], ident_f32[:])
-            result = e_stage.tile([P, FEATURES], F32)
+            result = e_stage.tile([P, FEATURES], F32, name="result")
             nc.scalar.copy(out=result[:], in_=out_ps[:])
             nc.sync.dma_start(out=out[j * P : (j + 1) * P, :], in_=result[:])
 
         h_at_tile = {0: 3, 1: 4, 2: 5, 4: 6, 5: 7, 6: 8}
-        scale_weights(0)
         multiply(0, range(BANKS))
-        h_transposes(h_at_tile[0])
-        for j in range(TILES + 3):
-            if j + 1 < TILES:
-                scale_weights(j + 1)
+        h_mirror_transposes(h_at_tile[0])
+        BY_VECTOR = 2
+        for j in range(TILES + 2):
             if 2 <= j < TILES + 2:
                 rho_transpose(j - 2)
-            if j >= 3:
+            if 3 <= j < TILES + 3 - BY_VECTOR:
                 add_views(j - 3, 0)
             if 2 <= j < TILES + 2:
                 rho_times_w2(j - 2)
-            if j >= 3:
+            if 3 <= j < TILES + 3 - BY_VECTOR:
                 add_views(j - 3, 1)
             if j + 1 < TILES:
                 multiply(j + 1, range(BANKS))
-            if j >= 3:
+            if 3 <= j < TILES + 3 - BY_VECTOR:
                 turn_back_and_store(j - 3)
             if j + 1 in h_at_tile:
-                h_transposes(h_at_tile[j + 1])
+                if h_at_tile[j + 1] in direct:
+                    h_transposes(h_at_tile[j + 1])
+                else:
+                    h_mirror_transposes(h_at_tile[j + 1])
             if j in h_at_tile:
-                h_sum(h_at_tile[j])
+                if h_at_tile[j] in direct:
+                    h_sum(h_at_tile[j])
+                else:
+                    h_mirror_copy(h_at_tile[j])
             if j < TILES:
                 weigh(j)
                 product(j)
-            if j in h_at_tile:
+            if j in h_at_tile and h_at_tile[j] in direct:
                 h_mask(h_at_tile[j])
             if 2 <= j < TILES + 2:
                 correct(j - 2)
+                if j - 2 >= TILES - BY_VECTOR:
+                    finish_last(j - 2)
+            if TILES - BY_VECTOR <= j - 1 < TILES:
+                sum_views(j - 1)
             if 1 <= j < TILES + 1:
                 accumulate(j - 1)
             if j in h_at_tile:

@@ -173,7 +173,8 @@ def tile_graphlearner_v_kernel(tc, features, weight_tensor, similarity, grad_out
 
         def c_group(i):
             c_groupeds[i] = c_stage.tile([P, BANK, PACK], BF16, align_bytes=64, name="c_grouped")
-            nc.vector.tensor_copy(
+            copy = nc.scalar.copy if i % 4 == 2 else nc.vector.tensor_copy
+            copy(
                 out=c_groupeds[i][:].rearrange("p (c i) t -> p c t i", i=4),
                 in_=c_plains[i][:].rearrange("p t (c i) -> p c t i", i=4),
             )

@@ -280,7 +280,7 @@ def tile_graphlearner_v_kernel(tc, features, weight_tensor, similarity, grad_out
             rho_pad = keep.tile([P, P], F32, name="rho_pad%d" % i)
             nc.vector.memset(rho_pad[:], 0.0)
             rho_pads.append(rho_pad)
-        view_sums = {}
+        view_sums, f_pss = {}, {}
         dc, terms, prods, smalls, rhoTs, corrections, outT_pss, outTs = {}, {}, {}, {}, {}, {}, {}, {}
 
         def multiply(j, banks):
@@ -317,7 +317,7 @@ def tile_graphlearner_v_kernel(tc, features, weight_tensor, similarity, grad_out
             lo = c_stage.tile([P, VIEWS // 2, FEATURES], F32, tag="c_plain", name="prod_lo")
             hi = c_stage.tile([P, VIEWS // 2, FEATURES], F32, tag="c_grouped", name="prod_hi", align_bytes=64)
             prods[j] = (lo, hi)
-            for b in range(BANKS):
+            for b in range(BANKS - vector_banks.get(j, 0)):
                 nc.gpsimd.tensor_tensor(
                     out=prods[j][b // 2][:, 2 * (b % 2) : 2 * (b % 2) + 2, :],
                     in0=terms[j][:, 2 * b : 2 * b + 2, :],
@@ -325,9 +325,27 @@ def tile_graphlearner_v_kernel(tc, features, weight_tensor, similarity, grad_out
                     op=ALU.mult,
                 )
 
+        def features_to_psum(j):
+            f_pss[j] = ps_turn.tile([P, FEATURES], BF16, tag="turn", name="f_ps")
+            for h in range(HALVES):
+                nc.tensor.transpose(f_pss[j][:, h * P : (h + 1) * P], fT[:, h, j, :], ident_bf[:])
+
+        def project(j):
+            unread = e_stage.tile([P, FEATURES], F32, name="unread_f32")
+            for v in range(VIEWS - VIEWS_PER_BANK * vector_banks[j], VIEWS):
+                nc.vector.scalar_tensor_tensor(
+                    out=unread[:],
+                    in0=f_pss[j][:],
+                    scalar=rn2[:, j * VIEWS + v : j * VIEWS + v + 1],
+                    in1=terms[j][:, v, :],
+                    op0=ALU.mult,
+                    op1=ALU.mult,
+                    accum_out=rho_pads[j % 2][:, v : v + 1],
+                )
+
         def accumulate(j):
             unread = e_stage.tile([P, FEATURES], BF16, name="unread")
-            for v in range(VIEWS):
+            for v in range(VIEWS - VIEWS_PER_BANK * vector_banks.get(j, 0)):
                 nc.scalar.activation(
                     out=unread[:],
                     in_=prods[j][v // 4][:, v % 4, :],
@@ -408,6 +426,8 @@ def tile_graphlearner_v_kernel(tc, features, weight_tensor, similarity, grad_out
         multiply(0, range(BANKS))
         h_mirror_transposes(h_at_tile[0])
         BY_VECTOR = 2
+        vector_banks = {0: 1, 3: 2, 4: 1, 5: 1, 7: 2, 8: 2, 9: 2, 10: 1, 11: 1}
+        features_to_psum(0)
         for j in range(TILES + 2):
             if 2 <= j < TILES + 2:
                 rho_transpose(j - 2)
@@ -419,6 +439,8 @@ def tile_graphlearner_v_kernel(tc, features, weight_tensor, similarity, grad_out
                 add_views(j - 3, 1)
             if j + 1 < TILES:
                 multiply(j + 1, range(BANKS))
+            if j + 1 in vector_banks:
+                features_to_psum(j + 1)
             if 3 <= j < TILES + 3 - BY_VECTOR:
                 turn_back_and_store(j - 3)
             if j + 1 in h_at_tile:
@@ -434,6 +456,8 @@ def tile_graphlearner_v_kernel(tc, features, weight_tensor, similarity, grad_out
             if j < TILES:
                 weigh(j)
                 product(j)
+                if j in vector_banks:
+                    project(j)
             if j in h_at_tile and h_at_tile[j] in direct:
                 h_mask(h_at_tile[j])
             if 2 <= j < TILES + 2:

@@ -28,14 +28,14 @@ BANKS = COLUMNS // BANK
 VIEWS_PER_BANK = BANK // FEATURES
 THRESHOLD = 0.65
 EPS = 1e-12
-SIM_AHEAD = 3
+SIM_AHEAD = 2
 
 
 def tile_graphlearner_v_kernel(tc, features, weight_tensor, similarity, grad_out, out):
     nc = tc.nc
     with ExitStack() as stack:
         keep = stack.enter_context(tc.tile_pool(name="keep", bufs=1))
-        c_stage = stack.enter_context(tc.tile_pool(name="c_stage", bufs=2))
+        c_stage = stack.enter_context(tc.tile_pool(name="c_stage", bufs=3))
         sim_pool = stack.enter_context(tc.tile_pool(name="sim_pool", bufs=SIM_AHEAD))
         h_stage = stack.enter_context(tc.tile_pool(name="h_stage", bufs=2))
         e_stage = stack.enter_context(tc.tile_pool(name="e_stage", bufs=2))
@@ -137,7 +137,9 @@ def tile_graphlearner_v_kernel(tc, features, weight_tensor, similarity, grad_out
             nc.vector.tensor_scalar_max(out=norm[:, cols], in0=norm[:, cols], scalar1=EPS)
             nc.vector.reciprocal(out=rn[:, cols], in_=norm[:, cols])
             nc.vector.tensor_scalar_mul(out=rn8[:, cols], in0=rn[:, cols], scalar1=1.0 / VIEWS)
-            nc.vector.tensor_tensor(out=rn2[:, cols], in0=rn[:, cols], in1=rn[:, cols], op=ALU.mult)
+            nc.vector.scalar_tensor_tensor(
+                out=rn2[:, cols], in0=rn[:, cols], scalar=-1.0, in1=rn[:, cols], op0=ALU.mult, op1=ALU.mult
+            )
 
         c_codes = keep.tile([P, PASSES, COLUMNS], U32, align_bytes=64)
         c_scales = keep.tile([P, PASSES, COLUMNS], U8, align_bytes=64)
@@ -367,14 +369,19 @@ def tile_graphlearner_v_kernel(tc, features, weight_tensor, similarity, grad_out
 
         def correct(j):
             corrections[j] = e_stage.tile([P, FEATURES], F32, name="correction")
-            nc.vector.scalar_tensor_tensor(
-                out=corrections[j][:],
-                in0=smalls[j][:, P:],
-                scalar=-1.0,
-                in1=f_bf[:, j, :],
-                op0=ALU.mult,
-                op1=ALU.mult,
-            )
+            if j >= TILES - BY_VECTOR:
+                nc.vector.scalar_tensor_tensor(
+                    out=corrections[j][:],
+                    in0=smalls[j][:, P:],
+                    scalar=1.0,
+                    in1=f_bf[:, j, :],
+                    op0=ALU.mult,
+                    op1=ALU.mult,
+                )
+            else:
+                weighted = e_stage.tile([P, FEATURES], F32, name="weighted")
+                nc.scalar.copy(out=weighted[:], in_=smalls[j][:, P:])
+                nc.gpsimd.tensor_tensor(out=corrections[j][:], in0=weighted[:], in1=f_bf[:, j, :], op=ALU.mult)
 
         def finish_last(j):
             result = e_stage.tile([P, FEATURES], F32, name="result")

from contextlib import ExitStack

import concourse.mybir as mybir
from concourse.masks import make_identity

FLOPS = 2 * 1536 * 1536 * 2048

BF16 = mybir.dt.bfloat16
F32 = mybir.dt.float32
U32 = mybir.dt.uint32
U8 = mybir.dt.uint8
E4M3X4 = mybir.dt.float8_e4m3fn_x4
E5M2X4 = mybir.dt.float8_e5m2_x4
ALU = mybir.AluOpType
ACT = mybir.ActivationFunctionType

P = 128
PACK = 4
TOKENS = 1536
TILES = TOKENS // P
PASSES = TOKENS // (P * PACK)
FEATURES = 256
HALVES = FEATURES // P
VIEWS = 8
COLUMNS = VIEWS * FEATURES
BANK = 512
BANKS = COLUMNS // BANK
VIEWS_PER_BANK = BANK // FEATURES
THRESHOLD = 0.65
EPS = 1e-12
SIM_AHEAD = 2


def tile_graphlearner_v_kernel(tc, features, weight_tensor, similarity, grad_out, out):
    nc = tc.nc
    with ExitStack() as stack:
        keep = stack.enter_context(tc.tile_pool(name="keep", bufs=1))
        c_stage = stack.enter_context(tc.tile_pool(name="c_stage", bufs=3))
        sim_pool = stack.enter_context(tc.tile_pool(name="sim_pool", bufs=SIM_AHEAD))
        h_stage = stack.enter_context(tc.tile_pool(name="h_stage", bufs=2))
        e_stage = stack.enter_context(tc.tile_pool(name="e_stage", bufs=2))
        t_stage = stack.enter_context(tc.tile_pool(name="t_stage", bufs=4))
        ps_bank = stack.enter_context(tc.psum_pool(name="ps_bank", bufs=4))
        ps_turn = stack.enter_context(tc.psum_pool(name="ps_turn", bufs=3))
        ps_small = stack.enter_context(tc.psum_pool(name="ps_small", bufs=1))

        warm = keep.tile([P, 1], F32)
        nc.vector.memset(warm[:], 1.0)
        nc.scalar.activation(out=warm[:], in_=warm[:], func=ACT.Sqrt)

        f_bf = keep.tile([P, TILES, FEATURES], BF16)
        nc.sync.dma_start(out=f_bf[:], in_=features.rearrange("(t p) d -> p t d", p=P))
        w_rows = keep.tile([P, FEATURES], BF16)
        nc.vector.memset(w_rows[:], 0.0)
        nc.sync.dma_start(out=w_rows[0:VIEWS, :], in_=weight_tensor)
        g_bf = keep.tile([P, TILES, TOKENS], BF16)
        g_view = grad_out.rearrange("(t p) c -> p t c", p=P)
        for g in range(PASSES):
            rows = slice(g * PACK, (g + 1) * PACK)
            nc.sync.dma_start(out=g_bf[:, rows, :], in_=g_view[:, rows, :])

        blocks = [(G, C) for C in range(PASSES) for G in range(PASSES)]
        direct = [u for u in range(len(blocks)) if blocks[u][0] >= blocks[u][1]]
        sims = {}

        def load_similarity(k):
            G, C = blocks[direct[k]]
            sim_sb = sim_pool.tile([P, PACK, BANK], F32)
            nc.sync.dma_start(
                out=sim_sb[:],
                in_=similarity[G * BANK : (G + 1) * BANK, C * BANK : (C + 1) * BANK].rearrange(
                    "(t p) n -> p t n", p=P
                ),
            )
            sims[direct[k]] = sim_sb

        for k in range(SIM_AHEAD):
            load_similarity(k)
        w_all = keep.tile([P, COLUMNS], BF16)
        nc.sync.dma_start(
            out=w_all[:], in_=weight_tensor.rearrange("v d -> (v d)").partition_broadcast(P)
        )

        ident_bf = keep.tile([P, P], BF16)
        make_identity(nc, ident_bf[:])
        ident_f32 = keep.tile([P, P], F32)
        make_identity(nc, ident_f32[:])

        wT_ps = ps_turn.tile([P, HALVES, P], BF16, tag="turn")
        for h in range(HALVES):
            nc.tensor.transpose(wT_ps[:, h, :], w_rows[:, h * P : (h + 1) * P], ident_bf[:])
        wT = keep.tile([P, HALVES, VIEWS], F32)
        nc.vector.tensor_copy(out=wT[:], in_=wT_ps[:, :, 0:VIEWS])
        w2T = keep.tile([P, HALVES, VIEWS], F32)
        nc.vector.tensor_tensor(out=w2T[:], in0=wT[:], in1=wT[:], op=ALU.mult)
        w_diag = keep.tile([P, HALVES, VIEWS, P], BF16)
        for h in range(HALVES):
            nc.vector.tensor_tensor(
                out=w_diag[:, h, :, :],
                in0=ident_bf[:].unsqueeze(1).to_broadcast([P, VIEWS, P]),
                in1=wT[:, h, :].unsqueeze(2).to_broadcast([P, VIEWS, P]),
                op=ALU.mult,
            )
        w2_rows = keep.tile([P, FEATURES], F32)
        nc.vector.tensor_tensor(out=w2_rows[:], in0=w_rows[:], in1=w_rows[:], op=ALU.mult)

        fT = keep.tile([P, HALVES, TILES, P], BF16)
        norm = keep.tile([P, TILES * VIEWS], F32)
        rn = keep.tile([P, TILES * VIEWS], F32)
        rn8 = keep.tile([P, TILES * VIEWS], F32)
        rn2 = keep.tile([P, TILES * VIEWS], F32)
        for g in range(PASSES):
            tiles = slice(g * PACK, (g + 1) * PACK)
            fT_ps = ps_bank.tile([P, HALVES, PACK, P], BF16, tag="bank")
            for h in range(HALVES):
                for t in range(PACK):
                    nc.tensor.transpose(
                        fT_ps[:, h, t, :], f_bf[:, g * PACK + t, h * P : (h + 1) * P], ident_bf[:]
                    )
            nc.scalar.copy(out=fT[:, :, tiles, :], in_=fT_ps[:])
            f2T = e_stage.tile([P, HALVES, PACK, P], F32, tag="scaled_w")
            nc.vector.tensor_tensor(
                out=f2T[:], in0=fT[:, :, tiles, :], in1=fT[:, :, tiles, :], op=ALU.mult
            )
            norm2 = ps_small.tile([P, PACK * VIEWS], F32, tag="small")
            for t in range(PACK):
                for h in range(HALVES):
                    nc.tensor.matmul(
                        out=norm2[:, t * VIEWS : (t + 1) * VIEWS],
                        lhsT=f2T[:, h, t, :],
                        rhs=w2T[:, h, :],
                        start=(h == 0),
                        stop=(h == HALVES - 1),
                    )
            cols = slice(g * PACK * VIEWS, (g + 1) * PACK * VIEWS)
            nc.scalar.activation(out=norm[:, cols], in_=norm2[:], func=ACT.Sqrt)
            nc.vector.tensor_scalar_max(out=norm[:, cols], in0=norm[:, cols], scalar1=EPS)
            nc.vector.reciprocal(out=rn[:, cols], in_=norm[:, cols])
            nc.vector.tensor_scalar_mul(out=rn8[:, cols], in0=rn[:, cols], scalar1=1.0 / VIEWS)
            nc.vector.scalar_tensor_tensor(
                out=rn2[:, cols], in0=rn[:, cols], scalar=-1.0, in1=rn[:, cols], op0=ALU.mult, op1=ALU.mult
            )

        c_codes = keep.tile([P, PASSES, COLUMNS], U32, align_bytes=64)
        c_scales = keep.tile([P, PASSES, COLUMNS], U8, align_bytes=64)
        h_codes = keep.tile([P, PASSES, TOKENS], U32, align_bytes=64)
        h_scales = keep.tile([P, PASSES, TOKENS], U8, align_bytes=64)

        def c_values(g, b, t, c_plain):
            fw = ps_bank.tile([P, VIEWS_PER_BANK, HALVES, P], F32, tag="bank")
            for h in range(HALVES):
                nc.tensor.matmul(
                    out=fw[:, :, h, :],
                    lhsT=fT[:, h, g * PACK + t, :],
                    rhs=w_diag[:, h, b * VIEWS_PER_BANK : (b + 1) * VIEWS_PER_BANK, :],
                    start=True,
                    stop=True,
                )
            for v in range(VIEWS_PER_BANK):
                col = (g * PACK + t) * VIEWS + b * VIEWS_PER_BANK + v
                nc.scalar.activation(
                    out=c_plain[:, t, v * FEATURES : (v + 1) * FEATURES],
                    in_=fw[:, v, :, :].rearrange("p h d -> p (h d)"),
                    func=ACT.Copy,
                    scale=rn[:, col : col + 1],
                )

        c_plains, c_groupeds, gTs, pair_sums, h_groupeds = {}, {}, {}, {}, {}

        def c_produce(i):
            g_c, b_c = divmod(i, BANKS)
            c_plains[i] = c_stage.tile([P, PACK, BANK], BF16, name="c_plain")
            for t in range(PACK):
                c_values(g_c, b_c, t, c_plains[i])

        def c_group(i):
            c_groupeds[i] = c_stage.tile([P, BANK, PACK], BF16, align_bytes=64, name="c_grouped")
            copy = nc.scalar.copy if i % 4 == 2 else nc.vector.tensor_copy
            copy(
                out=c_groupeds[i][:].rearrange("p (c i) t -> p c t i", i=4),
                in_=c_plains[i][:].rearrange("p t (c i) -> p c t i", i=4),
            )

        def c_quantise(i):
            g_c, b_c = divmod(i, BANKS)
            cols = slice(b_c * BANK, (b_c + 1) * BANK)
            nc.vector.quantize_mx(
                out=c_codes[:, g_c, cols].bitcast(E4M3X4),
                scales=c_scales[:, g_c, cols],
                in_=c_groupeds[i][:].rearrange("p c t -> p (c t)"),
            )

        def h_transposes(u):
            G, C = blocks[u]
            gTs[u] = []
            for half in range(2):
                gT_ps = ps_turn.tile([P, 2, PACK, P], BF16, tag="turn", name="gT_ps")
                for t2 in range(2):
                    m0 = (G * PACK + half * 2 + t2) * P
                    for jn in range(PACK):
                        nc.tensor.transpose(
                            gT_ps[:, t2, jn, :], g_bf[:, C * PACK + jn, m0 : m0 + P], ident_bf[:]
                        )
                gTs[u].append(gT_ps)

        def h_sum(u):
            G, C = blocks[u]
            pair_sums[u] = h_stage.tile([P, PACK, BANK], BF16, name="pair_sum")
            for half in range(2):
                nc.vector.tensor_tensor(
                    out=pair_sums[u][:, half * 2 : half * 2 + 2, :],
                    in0=g_bf[:, G * PACK + half * 2 : G * PACK + half * 2 + 2, C * BANK : (C + 1) * BANK],
                    in1=gTs[u][half][:].rearrange("p t j n -> p t (j n)"),
                    op=ALU.add,
                )

        def h_mask(u):
            if blocks[u][0] > blocks[u][1]:
                h_groupeds[u] = keep.tile([P, BANK, PACK], BF16, align_bytes=64, name="h_kept%d" % u)
            else:
                h_groupeds[u] = h_stage.tile([P, BANK, PACK], BF16, align_bytes=64, name="h_grouped")
            nc.vector.scalar_tensor_tensor(
                out=h_groupeds[u][:],
                in0=sims[u][:].rearrange("p t n -> p n t"),
                scalar=THRESHOLD,
                in1=pair_sums[u][:].rearrange("p t n -> p n t"),
                op0=ALU.is_gt,
                op1=ALU.mult,
            )
            if direct.index(u) + SIM_AHEAD < len(direct):
                load_similarity(direct.index(u) + SIM_AHEAD)

        def h_mirror_transposes(u):
            G, C = blocks[u]
            source = h_groupeds[blocks.index((C, G))]
            gTs[u] = []
            for half in range(2):
                hT_ps = ps_turn.tile([P, PACK, 2, P], BF16, tag="turn", name="hT_ps")
                for t2 in range(PACK):
                    for t in range(2):
                        nc.tensor.transpose(
                            hT_ps[:, t2, t, :], source[:, t2 * P : (t2 + 1) * P, half * 2 + t], ident_bf[:]
                        )
                gTs[u].append(hT_ps)

        def h_mirror_copy(u):
            h_groupeds[u] = h_stage.tile([P, BANK, PACK], BF16, align_bytes=64, name="h_grouped")
            for half in range(2):
                nc.scalar.copy(
                    out=h_groupeds[u][:, half * 2 * P : (half + 1) * 2 * P, :],
                    in_=gTs[u][half][:].rearrange("p m t n -> p (t n) m"),
                )

        def h_quantise(u):
            G, C = blocks[u]
            n_cols = slice(C * BANK, (C + 1) * BANK)
            nc.vector.quantize_mx(
                out=h_codes[:, G, n_cols].bitcast(E5M2X4),
                scales=h_scales[:, G, n_cols],
                in_=h_groupeds[u][:].rearrange("p n t -> p (n t)"),
            )

        h_at_step = {3: 0, 6: 1, 9: 2}
        c_produce(0)
        for i in range(TILES):
            if i + 1 < TILES:
                c_produce(i + 1)
            if i + 1 in h_at_step:
                h_transposes(h_at_step[i + 1])
            u = h_at_step.get(i)
            if u is not None:
                h_sum(u)
            c_group(i)
            if u is not None:
                h_mask(u)
            c_quantise(i)
            if u is not None:
                h_quantise(u)

        rho_pads = []
        for i in range(2):
            rho_pad = keep.tile([P, P], F32, name="rho_pad%d" % i)
            nc.vector.memset(rho_pad[:], 0.0)
            rho_pads.append(rho_pad)
        view_sums, f_pss = {}, {}
        dc, terms, prods, smalls, rhoTs, corrections, outT_pss, outTs = {}, {}, {}, {}, {}, {}, {}, {}

        def multiply(j, banks):
            n_cols = slice(j * P, (j + 1) * P)
            for b in banks:
                cols = slice(b * BANK, (b + 1) * BANK)
                bank = ps_bank.tile([P, BANK], F32, tag="bank", name="dc%d" % b)
                for g in range(PASSES):
                    nc.tensor.matmul_mx(
                        out=bank[:],
                        lhsT=h_codes[:, g, n_cols].bitcast(E5M2X4),
                        lhsT_scale=h_scales[:, g, n_cols],
                        rhs=c_codes[:, g, cols].bitcast(E4M3X4),
                        rhs_scale=c_scales[:, g, cols],
                        start=(g == 0),
                        stop=(g == PASSES - 1),
                    )
                dc[j, b] = bank

        def weigh(j):
            terms[j] = t_stage.tile([P, VIEWS, FEATURES], F32, name="terms")
            for v in range(VIEWS):
                b, half = divmod(v, VIEWS_PER_BANK)
                nc.vector.scalar_tensor_tensor(
                    out=terms[j][:, v, :],
                    in0=dc[j, b][:, half * FEATURES : (half + 1) * FEATURES],
                    scalar=rn8[:, j * VIEWS + v : j * VIEWS + v + 1],
                    in1=w_all[:, v * FEATURES : (v + 1) * FEATURES],
                    op0=ALU.mult,
                    op1=ALU.mult,
                )

        def product(j):
            lo = c_stage.tile([P, VIEWS // 2, FEATURES], F32, tag="c_plain", name="prod_lo")
            hi = c_stage.tile([P, VIEWS // 2, FEATURES], F32, tag="c_grouped", name="prod_hi", align_bytes=64)
            prods[j] = (lo, hi)
            for b in range(BANKS - vector_banks.get(j, 0)):
                nc.gpsimd.tensor_tensor(
                    out=prods[j][b // 2][:, 2 * (b % 2) : 2 * (b % 2) + 2, :],
                    in0=terms[j][:, 2 * b : 2 * b + 2, :],
                    in1=f_bf[:, j, :].unsqueeze(1).to_broadcast([P, 2, FEATURES]),
                    op=ALU.mult,
                )

        def features_to_psum(j):
            f_pss[j] = ps_turn.tile([P, FEATURES], BF16, tag="turn", name="f_ps")
            for h in range(HALVES):
                nc.tensor.transpose(f_pss[j][:, h * P : (h + 1) * P], fT[:, h, j, :], ident_bf[:])

        def project(j):
            unread = e_stage.tile([P, FEATURES], F32, name="unread_f32")
            for v in range(VIEWS - VIEWS_PER_BANK * vector_banks[j], VIEWS):
                nc.vector.scalar_tensor_tensor(
                    out=unread[:],
                    in0=f_pss[j][:],
                    scalar=rn2[:, j * VIEWS + v : j * VIEWS + v + 1],
                    in1=terms[j][:, v, :],
                    op0=ALU.mult,
                    op1=ALU.mult,
                    accum_out=rho_pads[j % 2][:, v : v + 1],
                )

        def accumulate(j):
            unread = e_stage.tile([P, FEATURES], BF16, name="unread")
            for v in range(VIEWS - VIEWS_PER_BANK * vector_banks.get(j, 0)):
                nc.scalar.activation(
                    out=unread[:],
                    in_=prods[j][v // 4][:, v % 4, :],
                    func=ACT.Copy,
                    scale=rn2[:, j * VIEWS + v : j * VIEWS + v + 1],
                    accum_out=rho_pads[j % 2][:, v : v + 1],
                )

        def rho_transpose(j):
            smalls[j] = ps_small.tile([P, P + FEATURES], F32, tag="small", name="small")
            nc.tensor.transpose(smalls[j][:, 0:P], rho_pads[j % 2][:], ident_f32[:])
            rhoTs[j] = e_stage.tile([P, P], F32, name="rhoT")
            nc.scalar.copy(out=rhoTs[j][:], in_=smalls[j][:, 0:P])

        def rho_times_w2(j):
            nc.tensor.matmul(
                out=smalls[j][:, P:], lhsT=rhoTs[j][:], rhs=w2_rows[:], start=True, stop=True
            )

        def correct(j):
            corrections[j] = e_stage.tile([P, FEATURES], F32, name="correction")
            if j >= TILES - BY_VECTOR:
                nc.vector.scalar_tensor_tensor(
                    out=corrections[j][:],
                    in0=smalls[j][:, P:],
                    scalar=1.0,
                    in1=f_bf[:, j, :],
                    op0=ALU.mult,
                    op1=ALU.mult,
                )
            else:
                weighted = e_stage.tile([P, FEATURES], F32, name="weighted")
                nc.scalar.copy(out=weighted[:], in_=smalls[j][:, P:])
                nc.gpsimd.tensor_tensor(out=corrections[j][:], in0=weighted[:], in1=f_bf[:, j, :], op=ALU.mult)

        def finish_last(j):
            result = e_stage.tile([P, FEATURES], F32, name="result")
            nc.vector.tensor_tensor(out=result[:], in0=view_sums[j][:], in1=corrections[j][:], op=ALU.add)
            nc.sync.dma_start(out=out[j * P : (j + 1) * P, :], in_=result[:])

        def sum_views(j):
            sum4 = e_stage.tile([P, 4, FEATURES], F32, tag="scaled_w", name="sum4")
            nc.vector.tensor_tensor(out=sum4[:], in0=terms[j][:, 0:4, :], in1=terms[j][:, 4:8, :], op=ALU.add)
            sum2 = e_stage.tile([P, 2, FEATURES], F32, name="sum2")
            nc.vector.tensor_tensor(out=sum2[:], in0=sum4[:, 0:2, :], in1=sum4[:, 2:4, :], op=ALU.add)
            view_sums[j] = e_stage.tile([P, FEATURES], F32, name="view_sum")
            nc.vector.tensor_tensor(out=view_sums[j][:], in0=sum2[:, 0, :], in1=sum2[:, 1, :], op=ALU.add)

        def add_views(j, h):
            if h == 0:
                outT_pss[j] = ps_turn.tile([P, HALVES, P], F32, tag="turn", name="outT_ps")
            d_cols = slice(h * P, (h + 1) * P)
            for v in range(VIEWS):
                nc.tensor.matmul(
                    out=outT_pss[j][:, h, :],
                    lhsT=terms[j][:, v, d_cols],
                    rhs=ident_f32[:],
                    is_transpose=True,
                    start=(v == 0),
                    stop=False,
                )
            nc.tensor.matmul(
                out=outT_pss[j][:, h, :],
                lhsT=corrections[j][:, d_cols],
                rhs=ident_f32[:],
                is_transpose=True,
                start=False,
                stop=True,
            )
            if h == HALVES - 1:
                outTs[j] = e_stage.tile([P, HALVES, P], F32, name="outT")
                nc.scalar.copy(out=outTs[j][:], in_=outT_pss[j][:])

        def turn_back_and_store(j):
            out_ps = ps_turn.tile([P, FEATURES], F32, tag="turn", name="out_ps")
            for h in range(HALVES):
                nc.tensor.transpose(out_ps[:, h * P : (h + 1) * P], outTs[j][:, h, :], ident_f32[:])
            result = e_stage.tile([P, FEATURES], F32, name="result")
            nc.scalar.copy(out=result[:], in_=out_ps[:])
            nc.sync.dma_start(out=out[j * P : (j + 1) * P, :], in_=result[:])

        h_at_tile = {0: 3, 1: 4, 2: 5, 4: 6, 5: 7, 6: 8}
        multiply(0, range(BANKS))
        h_mirror_transposes(h_at_tile[0])
        BY_VECTOR = 2
        vector_banks = {0: 1, 3: 2, 4: 1, 5: 1, 7: 2, 8: 2, 9: 2, 10: 1, 11: 1}
        features_to_psum(0)
        for j in range(TILES + 2):
            if 2 <= j < TILES + 2:
                rho_transpose(j - 2)
            if 3 <= j < TILES + 3 - BY_VECTOR:
                add_views(j - 3, 0)
            if 2 <= j < TILES + 2:
                rho_times_w2(j - 2)
            if 3 <= j < TILES + 3 - BY_VECTOR:
                add_views(j - 3, 1)
            if j + 1 < TILES:
                multiply(j + 1, range(BANKS))
            if j + 1 in vector_banks:
                features_to_psum(j + 1)
            if 3 <= j < TILES + 3 - BY_VECTOR:
                turn_back_and_store(j - 3)
            if j + 1 in h_at_tile:
                if h_at_tile[j + 1] in direct:
                    h_transposes(h_at_tile[j + 1])
                else:
                    h_mirror_transposes(h_at_tile[j + 1])
            if j in h_at_tile:
                if h_at_tile[j] in direct:
                    h_sum(h_at_tile[j])
                else:
                    h_mirror_copy(h_at_tile[j])
            if j < TILES:
                weigh(j)
                product(j)
                if j in vector_banks:
                    project(j)
            if j in h_at_tile and h_at_tile[j] in direct:
                h_mask(h_at_tile[j])
            if 2 <= j < TILES + 2:
                correct(j - 2)
                if j - 2 >= TILES - BY_VECTOR:
                    finish_last(j - 2)
            if TILES - BY_VECTOR <= j - 1 < TILES:
                sum_views(j - 1)
            if 1 <= j < TILES + 1:
                accumulate(j - 1)
            if j in h_at_tile:
                h_quantise(h_at_tile[j])
